import numpy as np
import ml_dtypes

BF16 = ml_dtypes.bfloat16


def bf(x):
    return np.asarray(x, np.float32).astype(BF16)


def f32(x):
    return np.asarray(x, np.float32)


def f64(x):
    return np.asarray(x).astype(np.float64)


def striped(idx):
    return np.tile(idx.reshape(-1, 16).T, (8, 1))


D, S, M, Q, P, N = 128, 2048, 256, 384, 128, 2048


def setup_inputs():
    return {"table": bf(np.random.standard_normal((D, S))), "w1": bf(np.random.standard_normal((D, M)) / np.sqrt(D)), "w2": bf(np.random.standard_normal((M, Q)) * np.sqrt(2.0 / M)), "dec_w": bf(np.random.standard_normal((Q, P)) / np.sqrt(Q)), "dec_b": f32(0.1 * np.random.standard_normal((P, 1))), "offs": striped(np.random.permutation(np.tile(np.arange(S), 2))[:N])}


def reference(table, w1, w2, dec_w, dec_b, offs):
    idx = offs[:16].T.reshape(-1)
    h = np.maximum(f64(w1).T @ f64(table)[:, idx], 0.0)
    x = f64(w2).T @ h
    return f64(dec_w).T @ x + f64(dec_b)

@@ -1,0 +1,75 @@
+import concourse.mybir as mybir
+
+BF16, F32, U16 = mybir.dt.bfloat16, mybir.dt.float32, mybir.dt.uint16
+RELU = mybir.ActivationFunctionType.Relu
+
+P = 128
+S = 2048
+N = 2048
+M_BLOCKS = 2
+Q_BLOCKS = 3
+PIECE = 512
+N_PIECES = N // PIECE
+PIECE_COLS = PIECE // 16
+
+FLOPS = 2 * N * (P * M_BLOCKS * P + M_BLOCKS * P * Q_BLOCKS * P + Q_BLOCKS * P * P)
+
+
+def tile_ghn_kernel(tc, table, w1, w2, dec_w, dec_b, offs, out):
+    nc = tc.nc
+    with (
+        tc.tile_pool(name="held", bufs=1) as held,
+        tc.tile_pool(name="work", bufs=N_PIECES) as work,
+        tc.psum_pool(name="psum", bufs=8) as psum,
+    ):
+        offsets = held.tile([P, N // 16], U16, name="offsets")
+        nc.sync.dma_start(offsets[:], offs)
+        table_sb = held.tile([P, S], BF16, name="table_sb")
+        nc.sync.dma_start(table_sb[:], table)
+        w1_sb = held.tile([P, M_BLOCKS * P], BF16, name="w1_sb")
+        nc.scalar.dma_start(w1_sb[:], w1)
+        w2_sb = held.tile([P, M_BLOCKS, Q_BLOCKS * P], BF16, name="w2_sb")
+        nc.scalar.dma_start(w2_sb[:], w2.rearrange("(m p) q -> p m q", p=P))
+        dec_w_sb = held.tile([P, Q_BLOCKS, P], BF16, name="dec_w_sb")
+        nc.gpsimd.dma_start(dec_w_sb[:], dec_w.rearrange("(q p) o -> p q o", p=P))
+        bias = held.tile([P, 1], F32, name="bias")
+        nc.gpsimd.dma_start(bias[:], dec_b)
+
+        h_sb = {}
+        for j in range(N_PIECES):
+            picked = table_sb[:].indirect(offsets[:, j * PIECE_COLS : (j + 1) * PIECE_COLS])
+            for m in range(M_BLOCKS):
+                h_ps = psum.tile([P, PIECE], F32, name="h_ps", tag="bank")
+                nc.tensor.matmul(h_ps[:], w1_sb[:, m * P : (m + 1) * P], picked, start=True, stop=True)
+                h_m = work.tile([P, PIECE], BF16, name=f"h{m}")
+                if m % 2 == 0:
+                    nc.scalar.activation(h_m[:], h_ps[:], RELU)
+                else:
+                    nc.vector.tensor_scalar_max(h_m[:], h_ps[:], 0.0)
+                h_sb[j, m] = h_m
+
+        for j in range(N_PIECES):
+            x_sb = []
+            for q in range(Q_BLOCKS):
+                x_ps = psum.tile([P, PIECE], F32, name="x_ps", tag="bank")
+                for m in range(M_BLOCKS):
+                    nc.tensor.matmul(
+                        x_ps[:], w2_sb[:, m, q * P : (q + 1) * P], h_sb[j, m][:],
+                        start=(m == 0), stop=(m == M_BLOCKS - 1),
+                    )
+                x_q = work.tile([P, PIECE], BF16, name=f"x{q}")
+                if q % 2 == 0:
+                    nc.scalar.copy(x_q[:], x_ps[:])
+                else:
+                    nc.vector.tensor_copy(x_q[:], x_ps[:])
+                x_sb.append(x_q)
+
+            o_ps = psum.tile([P, PIECE], F32, name="o_ps", tag="bank")
+            for q in range(Q_BLOCKS):
+                nc.tensor.matmul(
+                    o_ps[:], dec_w_sb[:, q, :], x_sb[q][:],
+                    start=(q == 0), stop=(q == Q_BLOCKS - 1),
+                )
+            o_sb = work.tile([P, PIECE], F32, name="o_sb")
+            nc.vector.tensor_scalar_add(o_sb[:], o_ps[:], bias[:, 0:1])
+            nc.sync.dma_start(out[:, j * PIECE : (j + 1) * PIECE], o_sb[:])

@@ -11,6 +11,7 @@ Q_BLOCKS = 3
 PIECE = 512
 N_PIECES = N // PIECE
 PIECE_COLS = PIECE // 16
+WARM_UP = 6
 
 FLOPS = 2 * N * (P * M_BLOCKS * P + M_BLOCKS * P * Q_BLOCKS * P + Q_BLOCKS * P * P)
 
@@ -34,6 +35,12 @@ def tile_ghn_kernel(tc, table, w1, w2, dec_w, dec_b, offs, out):
         nc.gpsimd.dma_start(dec_w_sb[:], dec_w.rearrange("(q p) o -> p q o", p=P))
         bias = held.tile([P, 1], F32, name="bias")
         nc.gpsimd.dma_start(bias[:], dec_b)
+
+        zeros = held.tile([P, PIECE], BF16, name="zeros")
+        nc.vector.memset(zeros[:], 0.0)
+        warm_ps = psum.tile([P, PIECE], F32, name="warm_ps", tag="bank")
+        for i in range(WARM_UP):
+            nc.tensor.matmul(warm_ps[:], zeros[:, 0:P], zeros[:], start=True, stop=True)
 
         h_sb = {}
         for j in range(N_PIECES):

@@ -11,7 +11,7 @@ Q_BLOCKS = 3
 PIECE = 512
 N_PIECES = N // PIECE
 PIECE_COLS = PIECE // 16
-WARM_UP = 6
+TABLE_CHUNKS = 4
 
 FLOPS = 2 * N * (P * M_BLOCKS * P + M_BLOCKS * P * Q_BLOCKS * P + Q_BLOCKS * P * P)
 
@@ -25,22 +25,19 @@ def tile_ghn_kernel(tc, table, w1, w2, dec_w, dec_b, offs, out):
     ):
         offsets = held.tile([P, N // 16], U16, name="offsets")
         nc.sync.dma_start(offsets[:], offs)
-        table_sb = held.tile([P, S], BF16, name="table_sb")
-        nc.sync.dma_start(table_sb[:], table)
         w1_sb = held.tile([P, M_BLOCKS * P], BF16, name="w1_sb")
         nc.scalar.dma_start(w1_sb[:], w1)
+        table_sb = held.tile([P, S], BF16, name="table_sb")
+        for c in range(TABLE_CHUNKS):
+            queue = nc.sync if c % 2 == 0 else nc.scalar
+            columns = slice(c * (S // TABLE_CHUNKS), (c + 1) * (S // TABLE_CHUNKS))
+            queue.dma_start(table_sb[:, columns], table[:, columns])
         w2_sb = held.tile([P, M_BLOCKS, Q_BLOCKS * P], BF16, name="w2_sb")
-        nc.scalar.dma_start(w2_sb[:], w2.rearrange("(m p) q -> p m q", p=P))
+        nc.sync.dma_start(w2_sb[:], w2.rearrange("(m p) q -> p m q", p=P))
         dec_w_sb = held.tile([P, Q_BLOCKS, P], BF16, name="dec_w_sb")
         nc.gpsimd.dma_start(dec_w_sb[:], dec_w.rearrange("(q p) o -> p q o", p=P))
         bias = held.tile([P, 1], F32, name="bias")
         nc.gpsimd.dma_start(bias[:], dec_b)
-
-        zeros = held.tile([P, PIECE], BF16, name="zeros")
-        nc.vector.memset(zeros[:], 0.0)
-        warm_ps = psum.tile([P, PIECE], F32, name="warm_ps", tag="bank")
-        for i in range(WARM_UP):
-            nc.tensor.matmul(warm_ps[:], zeros[:, 0:P], zeros[:], start=True, stop=True)
 
         h_sb = {}
         for j in range(N_PIECES):

@@ -11,7 +11,6 @@ Q_BLOCKS = 3
 PIECE = 512
 N_PIECES = N // PIECE
 PIECE_COLS = PIECE // 16
-TABLE_CHUNKS = 4
 
 FLOPS = 2 * N * (P * M_BLOCKS * P + M_BLOCKS * P * Q_BLOCKS * P + Q_BLOCKS * P * P)
 
@@ -25,15 +24,12 @@ def tile_ghn_kernel(tc, table, w1, w2, dec_w, dec_b, offs, out):
     ):
         offsets = held.tile([P, N // 16], U16, name="offsets")
         nc.sync.dma_start(offsets[:], offs)
+        table_sb = held.tile([P, S], BF16, name="table_sb")
+        nc.sync.dma_start(table_sb[:], table)
         w1_sb = held.tile([P, M_BLOCKS * P], BF16, name="w1_sb")
         nc.scalar.dma_start(w1_sb[:], w1)
-        table_sb = held.tile([P, S], BF16, name="table_sb")
-        for c in range(TABLE_CHUNKS):
-            queue = nc.sync if c % 2 == 0 else nc.scalar
-            columns = slice(c * (S // TABLE_CHUNKS), (c + 1) * (S // TABLE_CHUNKS))
-            queue.dma_start(table_sb[:, columns], table[:, columns])
         w2_sb = held.tile([P, M_BLOCKS, Q_BLOCKS * P], BF16, name="w2_sb")
-        nc.sync.dma_start(w2_sb[:], w2.rearrange("(m p) q -> p m q", p=P))
+        nc.scalar.dma_start(w2_sb[:], w2.rearrange("(m p) q -> p m q", p=P))
         dec_w_sb = held.tile([P, Q_BLOCKS, P], BF16, name="dec_w_sb")
         nc.gpsimd.dma_start(dec_w_sb[:], dec_w.rearrange("(q p) o -> p q o", p=P))
         bias = held.tile([P, 1], F32, name="bias")
@@ -52,7 +48,7 @@ def tile_ghn_kernel(tc, table, w1, w2, dec_w, dec_b, offs, out):
                     nc.vector.tensor_scalar_max(h_m[:], h_ps[:], 0.0)
                 h_sb[j, m] = h_m
 
-        for j in range(N_PIECES):
+        def layer_2(j):
             x_sb = []
             for q in range(Q_BLOCKS):
                 x_ps = psum.tile([P, PIECE], F32, name="x_ps", tag="bank")
@@ -67,7 +63,9 @@ def tile_ghn_kernel(tc, table, w1, w2, dec_w, dec_b, offs, out):
                 else:
                     nc.vector.tensor_copy(x_q[:], x_ps[:])
                 x_sb.append(x_q)
+            return x_sb
 
+        def layer_3(j, x_sb):
             o_ps = psum.tile([P, PIECE], F32, name="o_ps", tag="bank")
             for q in range(Q_BLOCKS):
                 nc.tensor.matmul(
@@ -77,3 +75,10 @@ def tile_ghn_kernel(tc, table, w1, w2, dec_w, dec_b, offs, out):
             o_sb = work.tile([P, PIECE], F32, name="o_sb")
             nc.vector.tensor_scalar_add(o_sb[:], o_ps[:], bias[:, 0:1])
             nc.sync.dma_start(out[:, j * PIECE : (j + 1) * PIECE], o_sb[:])
+
+        x_before = layer_2(0)
+        for j in range(1, N_PIECES):
+            x_now = layer_2(j)
+            layer_3(j - 1, x_before)
+            x_before = x_now
+        layer_3(N_PIECES - 1, x_before)

@@ -2,6 +2,7 @@ import concourse.mybir as mybir
 
 BF16, F32, U16 = mybir.dt.bfloat16, mybir.dt.float32, mybir.dt.uint16
 RELU = mybir.ActivationFunctionType.Relu
+IDENTITY = mybir.ActivationFunctionType.Identity
 
 P = 128
 S = 2048
@@ -10,6 +11,7 @@ M_BLOCKS = 2
 Q_BLOCKS = 3
 PIECE = 512
 N_PIECES = N // PIECE
+HALF = PIECE // 2
 PIECE_COLS = PIECE // 16
 
 FLOPS = 2 * N * (P * M_BLOCKS * P + M_BLOCKS * P * Q_BLOCKS * P + Q_BLOCKS * P * P)
@@ -66,15 +68,20 @@ def tile_ghn_kernel(tc, table, w1, w2, dec_w, dec_b, offs, out):
             return x_sb
 
         def layer_3(j, x_sb):
-            o_ps = psum.tile([P, PIECE], F32, name="o_ps", tag="bank")
-            for q in range(Q_BLOCKS):
-                nc.tensor.matmul(
-                    o_ps[:], dec_w_sb[:, q, :], x_sb[q][:],
-                    start=(q == 0), stop=(q == Q_BLOCKS - 1),
-                )
-            o_sb = work.tile([P, PIECE], F32, name="o_sb")
-            nc.vector.tensor_scalar_add(o_sb[:], o_ps[:], bias[:, 0:1])
-            nc.sync.dma_start(out[:, j * PIECE : (j + 1) * PIECE], o_sb[:])
+            for half in range(2):
+                first = half * HALF
+                o_ps = psum.tile([P, HALF], F32, name="o_ps", tag="bank")
+                for q in range(Q_BLOCKS):
+                    nc.tensor.matmul(
+                        o_ps[:], dec_w_sb[:, q, :], x_sb[q][:, first : first + HALF],
+                        start=(q == 0), stop=(q == Q_BLOCKS - 1),
+                    )
+                o_sb = work.tile([P, HALF], F32, name=f"o{half}")
+                if half % 2 == 0:
+                    nc.scalar.activation(o_sb[:], o_ps[:], IDENTITY, bias=bias[:, 0:1])
+                else:
+                    nc.vector.tensor_scalar_add(o_sb[:], o_ps[:], bias[:, 0:1])
+                nc.sync.dma_start(out[:, j * PIECE + first : j * PIECE + first + HALF], o_sb[:])
 
         x_before = layer_2(0)
         for j in range(1, N_PIECES):

@@ -25,16 +25,16 @@ def tile_ghn_kernel(tc, table, w1, w2, dec_w, dec_b, offs, out):
         tc.psum_pool(name="psum", bufs=8) as psum,
     ):
         offsets = held.tile([P, N // 16], U16, name="offsets")
-        nc.sync.dma_start(offsets[:], offs)
         table_sb = held.tile([P, S], BF16, name="table_sb")
-        nc.sync.dma_start(table_sb[:], table)
         w1_sb = held.tile([P, M_BLOCKS * P], BF16, name="w1_sb")
-        nc.scalar.dma_start(w1_sb[:], w1)
         w2_sb = held.tile([P, M_BLOCKS, Q_BLOCKS * P], BF16, name="w2_sb")
-        nc.scalar.dma_start(w2_sb[:], w2.rearrange("(m p) q -> p m q", p=P))
         dec_w_sb = held.tile([P, Q_BLOCKS, P], BF16, name="dec_w_sb")
-        nc.gpsimd.dma_start(dec_w_sb[:], dec_w.rearrange("(q p) o -> p q o", p=P))
         bias = held.tile([P, 1], F32, name="bias")
+        nc.sync.dma_start(table_sb[:], table)
+        nc.sync.dma_start(offsets[:], offs)
+        nc.scalar.dma_start(w1_sb[:], w1)
+        nc.scalar.dma_start(w2_sb[:], w2.rearrange("(m p) q -> p m q", p=P))
+        nc.gpsimd.dma_start(dec_w_sb[:], dec_w.rearrange("(q p) o -> p q o", p=P))
         nc.gpsimd.dma_start(bias[:], dec_b)
 
         h_sb = {}

@@ -33,9 +33,12 @@ def tile_ghn_kernel(tc, table, w1, w2, dec_w, dec_b, offs, out):
         nc.sync.dma_start(table_sb[:], table)
         nc.sync.dma_start(offsets[:], offs)
         nc.scalar.dma_start(w1_sb[:], w1)
-        nc.scalar.dma_start(w2_sb[:], w2.rearrange("(m p) q -> p m q", p=P))
-        nc.gpsimd.dma_start(dec_w_sb[:], dec_w.rearrange("(q p) o -> p q o", p=P))
-        nc.gpsimd.dma_start(bias[:], dec_b)
+        nc.vector.tensor_copy(w2_sb[:, 0, 0:1], table_sb[:, 0:1])
+        nc.vector.tensor_copy(dec_w_sb[:, 0, 0:1], table_sb[:, 0:1])
+        nc.vector.tensor_copy(bias[:], table_sb[:, 0:1])
+        nc.sync.dma_start(w2_sb[:], w2.rearrange("(m p) q -> p m q", p=P))
+        nc.sync.dma_start(dec_w_sb[:], dec_w.rearrange("(q p) o -> p q o", p=P))
+        nc.sync.dma_start(bias[:], dec_b)
 
         h_sb = {}
         for j in range(N_PIECES):

@@ -12,6 +12,7 @@ Q_BLOCKS = 3
 PIECE = 512
 N_PIECES = N // PIECE
 HALF = PIECE // 2
+QUARTER = PIECE // 4
 PIECE_COLS = PIECE // 16
 
 FLOPS = 2 * N * (P * M_BLOCKS * P + M_BLOCKS * P * Q_BLOCKS * P + Q_BLOCKS * P * P)
@@ -70,25 +71,29 @@ def tile_ghn_kernel(tc, table, w1, w2, dec_w, dec_b, offs, out):
                 x_sb.append(x_q)
             return x_sb
 
-        def layer_3(j, x_sb):
-            for half in range(2):
-                first = half * HALF
-                o_ps = psum.tile([P, HALF], F32, name="o_ps", tag="bank")
+        def layer_3(j, x_sb, width):
+            for left in range(0, PIECE, 2 * width):
+                strips = (left, left + width)
+                o_ps = {}
+                for first in strips:
+                    o_ps[first] = psum.tile([P, width], F32, name="o_ps", tag="bank")
                 for q in range(Q_BLOCKS):
-                    nc.tensor.matmul(
-                        o_ps[:], dec_w_sb[:, q, :], x_sb[q][:, first : first + HALF],
-                        start=(q == 0), stop=(q == Q_BLOCKS - 1),
-                    )
-                o_sb = work.tile([P, HALF], F32, name=f"o{half}")
-                if half % 2 == 0:
-                    nc.scalar.activation(o_sb[:], o_ps[:], IDENTITY, bias=bias[:, 0:1])
-                else:
-                    nc.vector.tensor_scalar_add(o_sb[:], o_ps[:], bias[:, 0:1])
-                nc.sync.dma_start(out[:, j * PIECE + first : j * PIECE + first + HALF], o_sb[:])
+                    for first in strips:
+                        nc.tensor.matmul(
+                            o_ps[first][:], dec_w_sb[:, q, :], x_sb[q][:, first : first + width],
+                            start=(q == 0), stop=(q == Q_BLOCKS - 1),
+                        )
+                for first in strips:
+                    o_sb = work.tile([P, width], F32, name=f"o{first}")
+                    if first == left:
+                        nc.vector.tensor_scalar_add(o_sb[:], o_ps[first][:], bias[:, 0:1])
+                    else:
+                        nc.scalar.activation(o_sb[:], o_ps[first][:], IDENTITY, bias=bias[:, 0:1])
+                    nc.sync.dma_start(out[:, j * PIECE + first : j * PIECE + first + width], o_sb[:])
 
         x_before = layer_2(0)
         for j in range(1, N_PIECES):
             x_now = layer_2(j)
-            layer_3(j - 1, x_before)
+            layer_3(j - 1, x_before, HALF)
             x_before = x_now
-        layer_3(N_PIECES - 1, x_before)
+        layer_3(N_PIECES - 1, x_before, QUARTER)

@@ -31,9 +31,9 @@ def tile_ghn_kernel(tc, table, w1, w2, dec_w, dec_b, offs, out):
         w2_sb = held.tile([P, M_BLOCKS, Q_BLOCKS * P], BF16, name="w2_sb")
         dec_w_sb = held.tile([P, Q_BLOCKS, P], BF16, name="dec_w_sb")
         bias = held.tile([P, 1], F32, name="bias")
-        nc.sync.dma_start(table_sb[:], table)
+        nc.scalar.dma_start(table_sb[:], table)
         nc.sync.dma_start(offsets[:], offs)
-        nc.scalar.dma_start(w1_sb[:], w1)
+        nc.sync.dma_start(w1_sb[:], w1)
         nc.vector.tensor_copy(w2_sb[:, 0, 0:1], table_sb[:, 0:1])
         nc.vector.tensor_copy(dec_w_sb[:, 0, 0:1], table_sb[:, 0:1])
         nc.vector.tensor_copy(bias[:], table_sb[:, 0:1])

@@ -13,6 +13,8 @@ PIECE = 512
 N_PIECES = N // PIECE
 HALF = PIECE // 2
 QUARTER = PIECE // 4
+HALVES = (((0, HALF), (HALF, HALF)),)
+LAST_STRIPS = (((0, HALF),), ((HALF, QUARTER), (HALF + QUARTER, QUARTER)))
 PIECE_COLS = PIECE // 16
 
 FLOPS = 2 * N * (P * M_BLOCKS * P + M_BLOCKS * P * Q_BLOCKS * P + Q_BLOCKS * P * P)
@@ -71,21 +73,20 @@ def tile_ghn_kernel(tc, table, w1, w2, dec_w, dec_b, offs, out):
                 x_sb.append(x_q)
             return x_sb
 
-        def layer_3(j, x_sb, width):
-            for left in range(0, PIECE, 2 * width):
-                strips = (left, left + width)
+        def layer_3(j, x_sb, groups):
+            for strips in groups:
                 o_ps = {}
-                for first in strips:
+                for first, width in strips:
                     o_ps[first] = psum.tile([P, width], F32, name="o_ps", tag="bank")
                 for q in range(Q_BLOCKS):
-                    for first in strips:
+                    for first, width in strips:
                         nc.tensor.matmul(
                             o_ps[first][:], dec_w_sb[:, q, :], x_sb[q][:, first : first + width],
                             start=(q == 0), stop=(q == Q_BLOCKS - 1),
                         )
-                for first in strips:
+                for first, width in strips:
                     o_sb = work.tile([P, width], F32, name=f"o{first}")
-                    if first == left:
+                    if first % (2 * width) == 0:
                         nc.vector.tensor_scalar_add(o_sb[:], o_ps[first][:], bias[:, 0:1])
                     else:
                         nc.scalar.activation(o_sb[:], o_ps[first][:], IDENTITY, bias=bias[:, 0:1])
@@ -94,6 +95,6 @@ def tile_ghn_kernel(tc, table, w1, w2, dec_w, dec_b, offs, out):
         x_before = layer_2(0)
         for j in range(1, N_PIECES):
             x_now = layer_2(j)
-            layer_3(j - 1, x_before, HALF)
+            layer_3(j - 1, x_before, HALVES)
             x_before = x_now
-        layer_3(N_PIECES - 1, x_before, QUARTER)
+        layer_3(N_PIECES - 1, x_before, LAST_STRIPS)

import concourse.mybir as mybir

BF16, F32, U16 = mybir.dt.bfloat16, mybir.dt.float32, mybir.dt.uint16
RELU = mybir.ActivationFunctionType.Relu
IDENTITY = mybir.ActivationFunctionType.Identity

P = 128
S = 2048
N = 2048
M_BLOCKS = 2
Q_BLOCKS = 3
PIECE = 512
N_PIECES = N // PIECE
HALF = PIECE // 2
QUARTER = PIECE // 4
HALVES = (((0, HALF), (HALF, HALF)),)
LAST_STRIPS = (((0, HALF),), ((HALF, QUARTER), (HALF + QUARTER, QUARTER)))
PIECE_COLS = PIECE // 16

FLOPS = 2 * N * (P * M_BLOCKS * P + M_BLOCKS * P * Q_BLOCKS * P + Q_BLOCKS * P * P)


def tile_ghn_kernel(tc, table, w1, w2, dec_w, dec_b, offs, out):
    nc = tc.nc
    with (
        tc.tile_pool(name="held", bufs=1) as held,
        tc.tile_pool(name="work", bufs=N_PIECES) as work,
        tc.psum_pool(name="psum", bufs=8) as psum,
    ):
        offsets = held.tile([P, N // 16], U16, name="offsets")
        table_sb = held.tile([P, S], BF16, name="table_sb")
        w1_sb = held.tile([P, M_BLOCKS * P], BF16, name="w1_sb")
        w2_sb = held.tile([P, M_BLOCKS, Q_BLOCKS * P], BF16, name="w2_sb")
        dec_w_sb = held.tile([P, Q_BLOCKS, P], BF16, name="dec_w_sb")
        bias = held.tile([P, 1], F32, name="bias")
        nc.scalar.dma_start(table_sb[:], table)
        nc.sync.dma_start(offsets[:], offs)
        nc.sync.dma_start(w1_sb[:], w1)
        nc.vector.tensor_copy(w2_sb[:, 0, 0:1], table_sb[:, 0:1])
        nc.vector.tensor_copy(dec_w_sb[:, 0, 0:1], table_sb[:, 0:1])
        nc.vector.tensor_copy(bias[:], table_sb[:, 0:1])
        nc.sync.dma_start(w2_sb[:], w2.rearrange("(m p) q -> p m q", p=P))
        nc.sync.dma_start(dec_w_sb[:], dec_w.rearrange("(q p) o -> p q o", p=P))
        nc.sync.dma_start(bias[:], dec_b)

        h_sb = {}
        for j in range(N_PIECES):
            picked = table_sb[:].indirect(offsets[:, j * PIECE_COLS : (j + 1) * PIECE_COLS])
            for m in range(M_BLOCKS):
                h_ps = psum.tile([P, PIECE], F32, name="h_ps", tag="bank")
                nc.tensor.matmul(h_ps[:], w1_sb[:, m * P : (m + 1) * P], picked, start=True, stop=True)
                h_m = work.tile([P, PIECE], BF16, name=f"h{m}")
                if m % 2 == 0:
                    nc.scalar.activation(h_m[:], h_ps[:], RELU)
                else:
                    nc.vector.tensor_scalar_max(h_m[:], h_ps[:], 0.0)
                h_sb[j, m] = h_m

        def layer_2(j):
            x_sb = []
            for q in range(Q_BLOCKS):
                x_ps = psum.tile([P, PIECE], F32, name="x_ps", tag="bank")
                for m in range(M_BLOCKS):
                    nc.tensor.matmul(
                        x_ps[:], w2_sb[:, m, q * P : (q + 1) * P], h_sb[j, m][:],
                        start=(m == 0), stop=(m == M_BLOCKS - 1),
                    )
                x_q = work.tile([P, PIECE], BF16, name=f"x{q}")
                if q % 2 == 0:
                    nc.scalar.copy(x_q[:], x_ps[:])
                else:
                    nc.vector.tensor_copy(x_q[:], x_ps[:])
                x_sb.append(x_q)
            return x_sb

        def layer_3(j, x_sb, groups):
            for strips in groups:
                o_ps = {}
                for first, width in strips:
                    o_ps[first] = psum.tile([P, width], F32, name="o_ps", tag="bank")
                for q in range(Q_BLOCKS):
                    for first, width in strips:
                        nc.tensor.matmul(
                            o_ps[first][:], dec_w_sb[:, q, :], x_sb[q][:, first : first + width],
                            start=(q == 0), stop=(q == Q_BLOCKS - 1),
                        )
                for first, width in strips:
                    o_sb = work.tile([P, width], F32, name=f"o{first}")
                    if first % (2 * width) == 0:
                        nc.vector.tensor_scalar_add(o_sb[:], o_ps[first][:], bias[:, 0:1])
                    else:
                        nc.scalar.activation(o_sb[:], o_ps[first][:], IDENTITY, bias=bias[:, 0:1])
                    nc.sync.dma_start(out[:, j * PIECE + first : j * PIECE + first + width], o_sb[:])

        x_before = layer_2(0)
        for j in range(1, N_PIECES):
            x_now = layer_2(j)
            layer_3(j - 1, x_before, HALVES)
            x_before = x_now
        layer_3(N_PIECES - 1, x_before, LAST_STRIPS)
